import numpy as np
import ml_dtypes


def mxq(x, axis, fmt="e4m3"):
    dtype, down = {"e4m3": (ml_dtypes.float8_e4m3fn, 7), "e5m2": (ml_dtypes.float8_e5m2, 14)}[fmt]
    v = np.moveaxis(np.asarray(x, np.float32).astype(ml_dtypes.bfloat16).astype(np.float64), axis, -1)
    blocks = v.reshape(v.shape[:-1] + (-1, 32))
    amax = np.abs(blocks).max(-1, keepdims=True)
    byte = np.maximum(np.where(amax > 0, np.frexp(amax)[1] - 1 + 127, 0) - down, 1)
    scale = np.exp2(byte - 127.0)
    codes = (blocks / scale).astype(np.float32).astype(dtype).astype(np.float64)
    return np.moveaxis((codes * scale).reshape(v.shape), -1, axis)


WIDE = False


def mx_kscale(k):
    if not WIDE:
        return np.ones(k)
    levels = np.array([10, -10, 5, -5, 0])
    a = np.random.permutation(np.resize(levels, k // 512 * 4)).reshape(k // 512, 4)
    idx = np.arange(k)
    return np.exp2(a[idx // 512, idx % 128 // 32])


BF16 = ml_dtypes.bfloat16


def bf(x):
    return np.asarray(x, np.float32).astype(BF16)


def f64(x):
    return np.asarray(x).astype(np.float64)


M, K, N = 8192, 512, 256


def setup_inputs():
    s = mx_kscale(K)
    return {"A": bf(np.tril(np.random.standard_normal((M, K))) * s),
            "B": bf(np.tril(np.random.standard_normal((K, N))) * 1.5 / np.sqrt(K) / s[:, None])}


def reference(A, B):
    return np.tril(mxq(f64(A), 1, "e4m3") @ mxq(f64(B), 0, "e4m3"))

@@ -1,0 +1,153 @@
+from contextlib import ExitStack
+
+import concourse.mybir as mybir
+from concourse.masks import make_identity
+
+BF16 = mybir.dt.bfloat16
+F32 = mybir.dt.float32
+U32 = mybir.dt.uint32
+U8 = mybir.dt.uint8
+FP8X4 = mybir.dt.float8_e4m3fn_x4
+
+M, K, N = 8192, 512, 256
+FLOPS = 2 * M * K * N
+
+P = 128
+PACK = 4
+HALVES = 2
+WORDS = K // 2 // HALVES
+
+ROWS_PER_PARTITION = 8
+CHUNK_ROWS = P * ROWS_PER_PARTITION
+CHUNKS = M // CHUNK_ROWS
+
+BANK_TILES = 2
+ROUND_TILES = 4
+ROUND_BANKS = ROUND_TILES // BANK_TILES
+ROUNDS_PER_CHUNK = ROWS_PER_PARTITION // ROUND_TILES
+ROUNDS = CHUNKS * ROUNDS_PER_CHUNK
+
+
+def tile_modelnew_t_kernel(tc, A, B, out):
+    nc = tc.nc
+    with ExitStack() as ctx:
+        const = ctx.enter_context(tc.tile_pool(name="const", bufs=1))
+        a_pool = ctx.enter_context(tc.tile_pool(name="a", bufs=CHUNKS))
+        c_pool = ctx.enter_context(tc.tile_pool(name="c", bufs=CHUNKS))
+        work = ctx.enter_context(tc.tile_pool(name="work", bufs=3))
+        flipped_psum = ctx.enter_context(tc.psum_pool(name="flipped", bufs=4))
+        product_psum = ctx.enter_context(tc.psum_pool(name="product", bufs=4))
+        ctx.enter_context(tc.manual_schedule())
+
+        b_rows = const.tile([P, PACK, N], BF16)
+        nc.sync.dma_start(
+            out=b_rows[:].rearrange("p (u e) n -> p u e n", u=HALVES),
+            in_=B.rearrange("(u p e) n -> p u e n", u=HALVES, p=P),
+        )
+        a_chunks = []
+        for c in range(CHUNKS):
+            a_chunk = a_pool.tile([P, ROWS_PER_PARTITION, K], BF16)
+            nc.sync.dma_start(
+                out=a_chunk[:],
+                in_=A[c * CHUNK_ROWS : (c + 1) * CHUNK_ROWS, :].rearrange(
+                    "(p i) k -> p i k", i=ROWS_PER_PARTITION
+                ),
+            )
+            a_chunks.append(a_chunk)
+
+        identity = const.tile([P, P], F32)
+        make_identity(nc, identity[:])
+
+        b_grouped = const.tile([P, N, PACK], BF16, align_bytes=64)
+        nc.vector.tensor_copy(out=b_grouped[:], in_=b_rows[:].rearrange("p t n -> p n t"))
+        b_codes = const.tile([P, N], U32, align_bytes=64)
+        b_scales = const.tile([P, N], U8, align_bytes=64)
+        nc.vector.quantize_mx(
+            out=b_codes[:].bitcast(FP8X4),
+            scales=b_scales[:],
+            in_=b_grouped[:].rearrange("p n t -> p (n t)"),
+        )
+
+        grouped_of = {}
+        codes_of = {}
+        scales_of = {}
+        c_chunks = {}
+
+        def row_tiles(r):
+            return r // ROUNDS_PER_CHUNK, (r % ROUNDS_PER_CHUNK) * ROUND_TILES
+
+        def transpose_and_group(r):
+            c, first = row_tiles(r)
+            grouped = work.tile([P, ROUND_TILES, P, PACK], BF16, align_bytes=64)
+            for b in range(ROUND_BANKS):
+                flipped = flipped_psum.tile([P, BANK_TILES, HALVES, P], F32)
+                for j in range(BANK_TILES):
+                    words = a_chunks[c][:, first + b * BANK_TILES + j, :].bitcast(F32)
+                    for u in range(HALVES):
+                        nc.tensor.transpose(
+                            flipped[:, j, u, :], words[:, u * WORDS : (u + 1) * WORDS], identity[:]
+                        )
+                target = grouped[:, b * BANK_TILES : (b + 1) * BANK_TILES, :, :].bitcast(F32)
+                source = flipped[:].rearrange("p j u m -> p j m u")
+                if (r * ROUND_BANKS + b) % 4 == 3:
+                    nc.scalar.copy(out=target, in_=source)
+                else:
+                    nc.vector.tensor_copy(out=target, in_=source)
+            grouped_of[r] = grouped
+
+        def quantise(r):
+            codes = work.tile([P, ROUND_TILES * P], U32, align_bytes=64)
+            scales = work.tile([P, ROUND_TILES * P], U8, align_bytes=64)
+            nc.vector.quantize_mx(
+                out=codes[:].bitcast(FP8X4),
+                scales=scales[:],
+                in_=grouped_of[r][:].rearrange("p j m t -> p (j m t)"),
+            )
+            codes_of[r] = codes
+            scales_of[r] = scales
+
+        def multiply_and_store(r):
+            c, first = row_tiles(r)
+            if first == 0:
+                c_chunk = c_pool.tile([P, ROWS_PER_PARTITION, N], F32)
+                c_chunks[c] = c_chunk
+            for b in range(ROUND_BANKS):
+                product = product_psum.tile([P, BANK_TILES, N], F32)
+                for j in range(BANK_TILES):
+                    m_cols = slice((b * BANK_TILES + j) * P, (b * BANK_TILES + j + 1) * P)
+                    nc.tensor.matmul_mx(
+                        out=product[:, j, :],
+                        lhsT=codes_of[r][:, m_cols].bitcast(FP8X4),
+                        lhsT_scale=scales_of[r][:, m_cols],
+                        rhs=b_codes[:].bitcast(FP8X4),
+                        rhs_scale=b_scales[:],
+                        start=True,
+                        stop=True,
+                    )
+                i0 = first + b * BANK_TILES
+                nc.scalar.copy(out=c_chunks[c][:, i0 : i0 + BANK_TILES, :], in_=product[:])
+            if first + ROUND_TILES == ROWS_PER_PARTITION:
+                if c * CHUNK_ROWS < N:
+                    nc.gpsimd.affine_select(
+                        out=c_chunks[c][:],
+                        in_=c_chunks[c][:],
+                        pattern=[[1, ROWS_PER_PARTITION], [-1, N]],
+                        compare_op=mybir.AluOpType.is_ge,
+                        fill=0.0,
+                        base=c * CHUNK_ROWS,
+                        channel_multiplier=ROWS_PER_PARTITION,
+                    )
+                nc.sync.dma_start(
+                    out=out[c * CHUNK_ROWS : (c + 1) * CHUNK_ROWS, :].rearrange(
+                        "(p i) n -> p i n", i=ROWS_PER_PARTITION
+                    ),
+                    in_=c_chunks[c][:],
+                )
+
+        for step in range(ROUNDS + 2):
+            if step < ROUNDS:
+                transpose_and_group(step)
+            if 1 <= step <= ROUNDS:
+                quantise(step - 1)
+            if step >= 2:
+                multiply_and_store(step - 2)

@@ -47,12 +47,14 @@ def tile_modelnew_t_kernel(tc, A, B, out):
         a_chunks = []
         for c in range(CHUNKS):
             a_chunk = a_pool.tile([P, ROWS_PER_PARTITION, K], BF16)
-            nc.sync.dma_start(
-                out=a_chunk[:],
-                in_=A[c * CHUNK_ROWS : (c + 1) * CHUNK_ROWS, :].rearrange(
-                    "(p i) k -> p i k", i=ROWS_PER_PARTITION
-                ),
+            a_rows = A[c * CHUNK_ROWS : (c + 1) * CHUNK_ROWS, :].rearrange(
+                "(p i) k -> p i k", i=ROWS_PER_PARTITION
             )
+            piece = ROUND_TILES if c == 0 else ROWS_PER_PARTITION
+            for i0 in range(0, ROWS_PER_PARTITION, piece):
+                nc.sync.dma_start(
+                    out=a_chunk[:, i0 : i0 + piece, :], in_=a_rows[:, i0 : i0 + piece, :]
+                )
             a_chunks.append(a_chunk)
 
         identity = const.tile([P, P], F32)
@@ -126,22 +128,24 @@ def tile_modelnew_t_kernel(tc, A, B, out):
                     )
                 i0 = first + b * BANK_TILES
                 nc.scalar.copy(out=c_chunks[c][:, i0 : i0 + BANK_TILES, :], in_=product[:])
-            if first + ROUND_TILES == ROWS_PER_PARTITION:
-                if c * CHUNK_ROWS < N:
-                    nc.gpsimd.affine_select(
-                        out=c_chunks[c][:],
-                        in_=c_chunks[c][:],
-                        pattern=[[1, ROWS_PER_PARTITION], [-1, N]],
-                        compare_op=mybir.AluOpType.is_ge,
-                        fill=0.0,
-                        base=c * CHUNK_ROWS,
-                        channel_multiplier=ROWS_PER_PARTITION,
-                    )
-                nc.sync.dma_start(
-                    out=out[c * CHUNK_ROWS : (c + 1) * CHUNK_ROWS, :].rearrange(
-                        "(p i) n -> p i n", i=ROWS_PER_PARTITION
-                    ),
+            done = first + ROUND_TILES
+            if done == ROWS_PER_PARTITION and c * CHUNK_ROWS < N:
+                nc.gpsimd.affine_select(
+                    out=c_chunks[c][:],
                     in_=c_chunks[c][:],
+                    pattern=[[1, ROWS_PER_PARTITION], [-1, N]],
+                    compare_op=mybir.AluOpType.is_ge,
+                    fill=0.0,
+                    base=c * CHUNK_ROWS,
+                    channel_multiplier=ROWS_PER_PARTITION,
+                )
+            piece = ROUND_TILES if c == CHUNKS - 1 else ROWS_PER_PARTITION
+            if done % piece == 0:
+                c_rows = out[c * CHUNK_ROWS : (c + 1) * CHUNK_ROWS, :].rearrange(
+                    "(p i) n -> p i n", i=ROWS_PER_PARTITION
+                )
+                nc.sync.dma_start(
+                    out=c_rows[:, done - piece : done, :], in_=c_chunks[c][:, done - piece : done, :]
                 )
 
         for step in range(ROUNDS + 2):

@@ -37,7 +37,6 @@ def tile_modelnew_t_kernel(tc, A, B, out):
         work = ctx.enter_context(tc.tile_pool(name="work", bufs=3))
         flipped_psum = ctx.enter_context(tc.psum_pool(name="flipped", bufs=4))
         product_psum = ctx.enter_context(tc.psum_pool(name="product", bufs=4))
-        ctx.enter_context(tc.manual_schedule())
 
         b_rows = const.tile([P, PACK, N], BF16)
         nc.sync.dma_start(
@@ -47,14 +46,12 @@ def tile_modelnew_t_kernel(tc, A, B, out):
         a_chunks = []
         for c in range(CHUNKS):
             a_chunk = a_pool.tile([P, ROWS_PER_PARTITION, K], BF16)
-            a_rows = A[c * CHUNK_ROWS : (c + 1) * CHUNK_ROWS, :].rearrange(
-                "(p i) k -> p i k", i=ROWS_PER_PARTITION
+            nc.sync.dma_start(
+                out=a_chunk[:],
+                in_=A[c * CHUNK_ROWS : (c + 1) * CHUNK_ROWS, :].rearrange(
+                    "(p i) k -> p i k", i=ROWS_PER_PARTITION
+                ),
             )
-            piece = ROUND_TILES if c == 0 else ROWS_PER_PARTITION
-            for i0 in range(0, ROWS_PER_PARTITION, piece):
-                nc.sync.dma_start(
-                    out=a_chunk[:, i0 : i0 + piece, :], in_=a_rows[:, i0 : i0 + piece, :]
-                )
             a_chunks.append(a_chunk)
 
         identity = const.tile([P, P], F32)
@@ -128,30 +125,25 @@ def tile_modelnew_t_kernel(tc, A, B, out):
                     )
                 i0 = first + b * BANK_TILES
                 nc.scalar.copy(out=c_chunks[c][:, i0 : i0 + BANK_TILES, :], in_=product[:])
-            done = first + ROUND_TILES
-            if done == ROWS_PER_PARTITION and c * CHUNK_ROWS < N:
-                nc.gpsimd.affine_select(
-                    out=c_chunks[c][:],
-                    in_=c_chunks[c][:],
-                    pattern=[[1, ROWS_PER_PARTITION], [-1, N]],
-                    compare_op=mybir.AluOpType.is_ge,
-                    fill=0.0,
-                    base=c * CHUNK_ROWS,
-                    channel_multiplier=ROWS_PER_PARTITION,
-                )
-            piece = ROUND_TILES if c == CHUNKS - 1 else ROWS_PER_PARTITION
-            if done % piece == 0:
-                c_rows = out[c * CHUNK_ROWS : (c + 1) * CHUNK_ROWS, :].rearrange(
-                    "(p i) n -> p i n", i=ROWS_PER_PARTITION
-                )
+            if first + ROUND_TILES == ROWS_PER_PARTITION:
+                if c * CHUNK_ROWS < N:
+                    nc.gpsimd.affine_select(
+                        out=c_chunks[c][:],
+                        in_=c_chunks[c][:],
+                        pattern=[[1, ROWS_PER_PARTITION], [-1, N]],
+                        compare_op=mybir.AluOpType.is_ge,
+                        fill=0.0,
+                        base=c * CHUNK_ROWS,
+                        channel_multiplier=ROWS_PER_PARTITION,
+                    )
                 nc.sync.dma_start(
-                    out=c_rows[:, done - piece : done, :], in_=c_chunks[c][:, done - piece : done, :]
+                    out=out[c * CHUNK_ROWS : (c + 1) * CHUNK_ROWS, :].rearrange(
+                        "(p i) n -> p i n", i=ROWS_PER_PARTITION
+                    ),
+                    in_=c_chunks[c][:],
                 )
 
-        for step in range(ROUNDS + 2):
-            if step < ROUNDS:
-                transpose_and_group(step)
-            if 1 <= step <= ROUNDS:
-                quantise(step - 1)
-            if step >= 2:
-                multiply_and_store(step - 2)
+        for r in range(ROUNDS):
+            transpose_and_group(r)
+            quantise(r)
+            multiply_and_store(r)

from contextlib import ExitStack

import concourse.mybir as mybir
from concourse.masks import make_identity

BF16 = mybir.dt.bfloat16
F32 = mybir.dt.float32
U32 = mybir.dt.uint32
U8 = mybir.dt.uint8
FP8X4 = mybir.dt.float8_e4m3fn_x4

M, K, N = 8192, 512, 256
FLOPS = 2 * M * K * N

P = 128
PACK = 4
HALVES = 2
WORDS = K // 2 // HALVES

ROWS_PER_PARTITION = 8
CHUNK_ROWS = P * ROWS_PER_PARTITION
CHUNKS = M // CHUNK_ROWS

BANK_TILES = 2
ROUND_TILES = 4
ROUND_BANKS = ROUND_TILES // BANK_TILES
ROUNDS_PER_CHUNK = ROWS_PER_PARTITION // ROUND_TILES
ROUNDS = CHUNKS * ROUNDS_PER_CHUNK


def tile_modelnew_t_kernel(tc, A, B, out):
    nc = tc.nc
    with ExitStack() as ctx:
        const = ctx.enter_context(tc.tile_pool(name="const", bufs=1))
        a_pool = ctx.enter_context(tc.tile_pool(name="a", bufs=CHUNKS))
        c_pool = ctx.enter_context(tc.tile_pool(name="c", bufs=CHUNKS))
        work = ctx.enter_context(tc.tile_pool(name="work", bufs=3))
        flipped_psum = ctx.enter_context(tc.psum_pool(name="flipped", bufs=4))
        product_psum = ctx.enter_context(tc.psum_pool(name="product", bufs=4))

        b_rows = const.tile([P, PACK, N], BF16)
        nc.sync.dma_start(
            out=b_rows[:].rearrange("p (u e) n -> p u e n", u=HALVES),
            in_=B.rearrange("(u p e) n -> p u e n", u=HALVES, p=P),
        )
        a_chunks = []
        for c in range(CHUNKS):
            a_chunk = a_pool.tile([P, ROWS_PER_PARTITION, K], BF16)
            nc.sync.dma_start(
                out=a_chunk[:],
                in_=A[c * CHUNK_ROWS : (c + 1) * CHUNK_ROWS, :].rearrange(
                    "(p i) k -> p i k", i=ROWS_PER_PARTITION
                ),
            )
            a_chunks.append(a_chunk)

        identity = const.tile([P, P], F32)
        make_identity(nc, identity[:])

        b_grouped = const.tile([P, N, PACK], BF16, align_bytes=64)
        nc.vector.tensor_copy(out=b_grouped[:], in_=b_rows[:].rearrange("p t n -> p n t"))
        b_codes = const.tile([P, N], U32, align_bytes=64)
        b_scales = const.tile([P, N], U8, align_bytes=64)
        nc.vector.quantize_mx(
            out=b_codes[:].bitcast(FP8X4),
            scales=b_scales[:],
            in_=b_grouped[:].rearrange("p n t -> p (n t)"),
        )

        grouped_of = {}
        codes_of = {}
        scales_of = {}
        c_chunks = {}

        def row_tiles(r):
            return r // ROUNDS_PER_CHUNK, (r % ROUNDS_PER_CHUNK) * ROUND_TILES

        def transpose_and_group(r):
            c, first = row_tiles(r)
            grouped = work.tile([P, ROUND_TILES, P, PACK], BF16, align_bytes=64)
            for b in range(ROUND_BANKS):
                flipped = flipped_psum.tile([P, BANK_TILES, HALVES, P], F32)
                for j in range(BANK_TILES):
                    words = a_chunks[c][:, first + b * BANK_TILES + j, :].bitcast(F32)
                    for u in range(HALVES):
                        nc.tensor.transpose(
                            flipped[:, j, u, :], words[:, u * WORDS : (u + 1) * WORDS], identity[:]
                        )
                target = grouped[:, b * BANK_TILES : (b + 1) * BANK_TILES, :, :].bitcast(F32)
                source = flipped[:].rearrange("p j u m -> p j m u")
                if (r * ROUND_BANKS + b) % 4 == 3:
                    nc.scalar.copy(out=target, in_=source)
                else:
                    nc.vector.tensor_copy(out=target, in_=source)
            grouped_of[r] = grouped

        def quantise(r):
            codes = work.tile([P, ROUND_TILES * P], U32, align_bytes=64)
            scales = work.tile([P, ROUND_TILES * P], U8, align_bytes=64)
            nc.vector.quantize_mx(
                out=codes[:].bitcast(FP8X4),
                scales=scales[:],
                in_=grouped_of[r][:].rearrange("p j m t -> p (j m t)"),
            )
            codes_of[r] = codes
            scales_of[r] = scales

        def multiply_and_store(r):
            c, first = row_tiles(r)
            if first == 0:
                c_chunk = c_pool.tile([P, ROWS_PER_PARTITION, N], F32)
                c_chunks[c] = c_chunk
            for b in range(ROUND_BANKS):
                product = product_psum.tile([P, BANK_TILES, N], F32)
                for j in range(BANK_TILES):
                    m_cols = slice((b * BANK_TILES + j) * P, (b * BANK_TILES + j + 1) * P)
                    nc.tensor.matmul_mx(
                        out=product[:, j, :],
                        lhsT=codes_of[r][:, m_cols].bitcast(FP8X4),
                        lhsT_scale=scales_of[r][:, m_cols],
                        rhs=b_codes[:].bitcast(FP8X4),
                        rhs_scale=b_scales[:],
                        start=True,
                        stop=True,
                    )
                i0 = first + b * BANK_TILES
                nc.scalar.copy(out=c_chunks[c][:, i0 : i0 + BANK_TILES, :], in_=product[:])
            if first + ROUND_TILES == ROWS_PER_PARTITION:
                if c * CHUNK_ROWS < N:
                    nc.gpsimd.affine_select(
                        out=c_chunks[c][:],
                        in_=c_chunks[c][:],
                        pattern=[[1, ROWS_PER_PARTITION], [-1, N]],
                        compare_op=mybir.AluOpType.is_ge,
                        fill=0.0,
                        base=c * CHUNK_ROWS,
                        channel_multiplier=ROWS_PER_PARTITION,
                    )
                nc.sync.dma_start(
                    out=out[c * CHUNK_ROWS : (c + 1) * CHUNK_ROWS, :].rearrange(
                        "(p i) n -> p i n", i=ROWS_PER_PARTITION
                    ),
                    in_=c_chunks[c][:],
                )

        for r in range(ROUNDS):
            transpose_and_group(r)
            quantise(r)
            multiply_and_store(r)
